import numpy as np
import ml_dtypes

BF16 = ml_dtypes.bfloat16


def bf(x):
    return np.asarray(x, np.float32).astype(BF16)


def f32(x):
    return np.asarray(x, np.float32)


def f64(x):
    return np.asarray(x).astype(np.float64)


def striped(idx):
    return np.tile(idx.reshape(-1, 16).T, (8, 1))


C, S, N = 1024, 2048, 1024
EPS = 1e-5


def setup_inputs():
    return {
        "obs_emb": f32(np.random.standard_normal((C, S))),
        "act": f32(np.random.standard_normal((C, N))),
        "type_act": f32(0.5 * np.random.standard_normal((C, 1))),
        "type_obs": f32(0.5 * np.random.standard_normal((C, 1))),
        "ln_g": f32(1.0 + 0.1 * np.random.standard_normal((C, 1))),
        "ln_b": f32(0.1 * np.random.standard_normal((C, 1))),
        "wq": bf(np.random.standard_normal((C, C)) / np.sqrt(C)),
        "bq": f32(0.1 * np.random.standard_normal((C, 1))),
        "wk": bf(np.random.standard_normal((C, C)) / np.sqrt(C)),
        "bk": f32(0.1 * np.random.standard_normal((C, 1))),
        "wv": bf(np.random.standard_normal((C, C)) / np.sqrt(C)),
        "bv": f32(0.1 * np.random.standard_normal((C, 1))),
        "offs": striped(np.random.permutation(np.tile(np.arange(S), 2))[:N]),
    }


def reference(obs_emb, act, type_act, type_obs, ln_g, ln_b, wq, bq, wk, bk, wv, bv, offs):
    idx = offs[:16].T.reshape(-1)
    x = f64(obs_emb)[:, idx] + (f64(act) + f64(type_act) + f64(type_obs))
    mu = x.mean(axis=0, keepdims=True)
    var = ((x - mu) ** 2).mean(axis=0, keepdims=True)
    h = (x - mu) / np.sqrt(var + EPS) * f64(ln_g) + f64(ln_b)
    qp = f64(wq).T @ h + f64(bq)
    kp = f64(wk).T @ h + f64(bk)
    vp = f64(wv).T @ h + f64(bv)
    return np.concatenate([x, qp, kp, vp], axis=0)

@@ -1,0 +1,165 @@
+import concourse.mybir as mybir
+
+F32 = mybir.dt.float32
+BF16 = mybir.dt.bfloat16
+U16 = mybir.dt.uint16
+ADD = mybir.AluOpType.add
+SUB = mybir.AluOpType.subtract
+MULT = mybir.AluOpType.mult
+FUNC = mybir.ActivationFunctionType
+
+P = 128
+C = 1024
+S = 2048
+N = 1024
+EPS = 1e-5
+CB = C // P
+PIECE = 512
+PIECES = N // PIECE
+OFFS_COLS = PIECE // 16
+MB = 3 * CB
+GROUP = 3
+GROUPS = MB // GROUP
+
+FLOPS = 2 * 3 * C * C * N
+
+
+def tile_transformerrope_b_kernel(
+    tc, obs_emb, act, type_act, type_obs, ln_g, ln_b, wq, bq, wk, bk, wv, bv, offs, out
+):
+    nc = tc.nc
+    with (
+        tc.tile_pool(name="held", bufs=1) as held,
+        tc.tile_pool(name="acts", bufs=CB) as acts,
+        tc.tile_pool(name="xs", bufs=PIECES * CB) as xs_pool,
+        tc.tile_pool(name="hs", bufs=PIECES * CB) as hs_pool,
+        tc.tile_pool(name="squares", bufs=3) as squares,
+        tc.tile_pool(name="sums", bufs=2) as sums,
+        tc.tile_pool(name="stats", bufs=1) as stats,
+        tc.tile_pool(name="centred", bufs=CB) as centred_pool,
+        tc.tile_pool(name="staging", bufs=2 * GROUP) as staging,
+        tc.psum_pool(name="moments", bufs=1) as moments,
+        tc.psum_pool(name="banks", bufs=2 * GROUP) as banks_pool,
+    ):
+        offsets = held.tile([P, N // 16], U16, name="offsets")
+        nc.sync.dma_start(offsets[:], offs)
+
+        def per_partition(vec):
+            return vec.rearrange("(a p) o -> p (a o)", p=P)
+
+        t_act = held.tile([P, CB], F32, name="t_act")
+        t_obs = held.tile([P, CB], F32, name="t_obs")
+        gain = held.tile([P, CB], F32, name="gain")
+        shift = held.tile([P, CB], F32, name="shift")
+        bias = held.tile([P, MB], F32, name="bias")
+        nc.scalar.dma_start(t_act[:], per_partition(type_act))
+        nc.scalar.dma_start(t_obs[:], per_partition(type_obs))
+        nc.scalar.dma_start(gain[:], per_partition(ln_g))
+        nc.scalar.dma_start(shift[:], per_partition(ln_b))
+        for i, vec in enumerate((bq, bk, bv)):
+            nc.scalar.dma_start(bias[:, i * CB : (i + 1) * CB], per_partition(vec))
+
+        def load_act(piece, b):
+            a = acts.tile([P, PIECE], F32, name="a")
+            nc.sync.dma_start(
+                a[:], act[b * P : (b + 1) * P, piece * PIECE : (piece + 1) * PIECE]
+            )
+            return a
+
+        tables = []
+        act_tiles = {}
+        for b in range(CB):
+            table = held.tile([P, S], F32, name="table%d" % b)
+            nc.sync.dma_start(table[:], obs_emb[b * P : (b + 1) * P, :])
+            tables.append(table)
+            act_tiles[(0, b)] = load_act(0, b)
+
+        weights = []
+        for i, w in enumerate((wq, wk, wv)):
+            w_tile = held.tile([P, CB, C], BF16, name="w%d" % i)
+            nc.sync.dma_start(w_tile[:], w.rearrange("(k p) m -> p k m", p=P))
+            weights.append(w_tile)
+
+        type_sum = held.tile([P, CB], F32, name="type_sum")
+        nc.vector.tensor_tensor(type_sum[:], t_act[:], t_obs[:], ADD)
+        averager = held.tile([P, P], F32, name="averager")
+        nc.vector.memset(averager[:], 1.0 / C)
+        eps = held.tile([P, 1], F32, name="eps")
+        nc.vector.memset(eps[:], EPS)
+
+        h_tiles = {}
+
+        def prepare(piece):
+            piece_offsets = offsets[:, piece * OFFS_COLS : (piece + 1) * OFFS_COLS]
+            cols = slice(piece * PIECE, (piece + 1) * PIECE)
+            x_tiles = []
+            for b in range(CB):
+                a = act_tiles[(piece, b)]
+                nc.scalar.activation(a[:], a[:], FUNC.Identity, bias=type_sum[:, b : b + 1])
+                x = xs_pool.tile([P, PIECE], F32, name="x")
+                nc.vector.tensor_tensor(x[:], tables[b][:].indirect(piece_offsets), a[:], ADD)
+                x_tiles.append(x)
+                sq = squares.tile([P, PIECE], F32, name="sq")
+                nc.scalar.activation(sq[:], x[:], FUNC.Square)
+                if b == 0:
+                    run_x, run_sq = x, sq
+                else:
+                    next_x = sums.tile([P, PIECE], F32, name="run_x")
+                    nc.vector.tensor_tensor(next_x[:], run_x[:], x[:], ADD)
+                    next_sq = sums.tile([P, PIECE], F32, name="run_sq")
+                    nc.vector.tensor_tensor(next_sq[:], run_sq[:], sq[:], ADD)
+                    run_x, run_sq = next_x, next_sq
+
+            mean = moments.tile([P, PIECE], F32, name="mean")
+            nc.tensor.matmul(mean[:], averager[:], run_x[:], start=True, stop=True)
+            mean_sq = moments.tile([P, PIECE], F32, name="mean_sq")
+            nc.tensor.matmul(mean_sq[:], averager[:], run_sq[:], start=True, stop=True)
+            sq_mean = stats.tile([P, PIECE], F32, name="sq_mean")
+            nc.scalar.activation(sq_mean[:], mean[:], FUNC.Square)
+            var = stats.tile([P, PIECE], F32, name="var")
+            nc.vector.tensor_tensor(var[:], mean_sq[:], sq_mean[:], SUB)
+            rstd = stats.tile([P, PIECE], F32, name="rstd")
+            nc.scalar.activation(rstd[:], var[:], FUNC.Abs_reciprocal_sqrt, bias=eps[:])
+
+            for b in range(CB):
+                centred = centred_pool.tile([P, PIECE], F32, name="centred")
+                nc.vector.tensor_tensor(centred[:], x_tiles[b][:], mean[:], SUB)
+                nc.vector.tensor_tensor(centred[:], centred[:], rstd[:], MULT)
+                h = hs_pool.tile([P, PIECE], BF16, name="h")
+                nc.scalar.activation(
+                    h[:], centred[:], FUNC.Identity,
+                    bias=shift[:, b : b + 1], scale=gain[:, b : b + 1],
+                )
+                h_tiles[(piece, b)] = h
+            for b in range(CB):
+                nc.sync.dma_start(out[b * P : (b + 1) * P, cols], x_tiles[b][:])
+
+        def project(piece, group):
+            cols = slice(piece * PIECE, (piece + 1) * PIECE)
+            blocks = range(group * GROUP, (group + 1) * GROUP)
+            banks = [banks_pool.tile([P, PIECE], F32, name="bank") for m in blocks]
+            for k in range(CB):
+                for m, bank in zip(blocks, banks):
+                    w_cols = slice((m % CB) * P, (m % CB + 1) * P)
+                    nc.tensor.matmul(
+                        bank[:], weights[m // CB][:, k, w_cols], h_tiles[(piece, k)][:],
+                        start=(k == 0), stop=(k == CB - 1),
+                    )
+            for m, bank in zip(blocks, banks):
+                staged = staging.tile([P, PIECE], F32, name="staged")
+                if m % GROUP == 1:
+                    nc.vector.tensor_scalar(staged[:], bank[:], bias[:, m : m + 1], None, ADD)
+                else:
+                    nc.scalar.activation(staged[:], bank[:], FUNC.Identity, bias=bias[:, m : m + 1])
+                nc.sync.dma_start(out[C + m * P : C + (m + 1) * P, cols], staged[:])
+
+        prepare(0)
+        for b in range(CB):
+            act_tiles[(1, b)] = load_act(1, b)
+        for group in range(GROUPS // 2):
+            project(0, group)
+        prepare(1)
+        for group in range(GROUPS // 2, GROUPS):
+            project(0, group)
+        for group in range(GROUPS):
+            project(1, group)

@@ -14,12 +14,13 @@ S = 2048
 N = 1024
 EPS = 1e-5
 CB = C // P
-PIECE = 512
+PIECE = 256
 PIECES = N // PIECE
 OFFS_COLS = PIECE // 16
 MB = 3 * CB
 GROUP = 3
 GROUPS = MB // GROUP
+SHARE = CB // (GROUPS // 2)
 
 FLOPS = 2 * 3 * C * C * N
 
@@ -30,55 +31,56 @@ def tile_transformerrope_b_kernel(
     nc = tc.nc
     with (
         tc.tile_pool(name="held", bufs=1) as held,
-        tc.tile_pool(name="acts", bufs=CB) as acts,
-        tc.tile_pool(name="xs", bufs=PIECES * CB) as xs_pool,
-        tc.tile_pool(name="hs", bufs=PIECES * CB) as hs_pool,
-        tc.tile_pool(name="squares", bufs=3) as squares,
-        tc.tile_pool(name="sums", bufs=2) as sums,
+        tc.tile_pool(name="gathered", bufs=2 * SHARE) as gathered_pool,
+        tc.tile_pool(name="pairs", bufs=2 * CB) as pairs,
+        tc.tile_pool(name="hs", bufs=2 * CB) as hs_pool,
+        tc.tile_pool(name="sums", bufs=3) as sums,
         tc.tile_pool(name="stats", bufs=1) as stats,
         tc.tile_pool(name="centred", bufs=CB) as centred_pool,
-        tc.tile_pool(name="staging", bufs=2 * GROUP) as staging,
-        tc.psum_pool(name="moments", bufs=1) as moments,
+        tc.tile_pool(name="staging", bufs=3) as staging,
+        tc.psum_pool(name="moments", bufs=2) as moments_pool,
         tc.psum_pool(name="banks", bufs=2 * GROUP) as banks_pool,
     ):
+        def piece_cols(piece):
+            return slice(piece * PIECE, (piece + 1) * PIECE)
+
         offsets = held.tile([P, N // 16], U16, name="offsets")
         nc.sync.dma_start(offsets[:], offs)
 
-        def per_partition(vec):
-            return vec.rearrange("(a p) o -> p (a o)", p=P)
-
-        t_act = held.tile([P, CB], F32, name="t_act")
-        t_obs = held.tile([P, CB], F32, name="t_obs")
-        gain = held.tile([P, CB], F32, name="gain")
-        shift = held.tile([P, CB], F32, name="shift")
+        channel_vectors = []
+        for i, vec in enumerate((type_act, type_obs, ln_g, ln_b)):
+            v_tile = held.tile([P, CB], F32, name="vec%d" % i)
+            nc.scalar.dma_start(v_tile[:], vec.rearrange("(p a) o -> p (a o)", a=CB))
+            channel_vectors.append(v_tile)
+        t_act, t_obs, gain, shift = channel_vectors
         bias = held.tile([P, MB], F32, name="bias")
-        nc.scalar.dma_start(t_act[:], per_partition(type_act))
-        nc.scalar.dma_start(t_obs[:], per_partition(type_obs))
-        nc.scalar.dma_start(gain[:], per_partition(ln_g))
-        nc.scalar.dma_start(shift[:], per_partition(ln_b))
         for i, vec in enumerate((bq, bk, bv)):
-            nc.scalar.dma_start(bias[:, i * CB : (i + 1) * CB], per_partition(vec))
-
-        def load_act(piece, b):
-            a = acts.tile([P, PIECE], F32, name="a")
-            nc.sync.dma_start(
-                a[:], act[b * P : (b + 1) * P, piece * PIECE : (piece + 1) * PIECE]
+            nc.scalar.dma_start(
+                bias[:, i * CB : (i + 1) * CB], vec.rearrange("(a p) o -> p (a o)", p=P)
             )
-            return a
 
+        act_blocks = act.rearrange("(p a) n -> p a n", a=CB)
+        obs_blocks = obs_emb.rearrange("(p a) s -> a p s", a=CB)
+        act_tiles = []
+        weights = []
+
+        def load_act(piece):
+            a_tile = held.tile([P, CB, PIECE], F32, name="act%d" % piece)
+            nc.sync.dma_start(a_tile[:], act_blocks[:, :, piece_cols(piece)])
+            act_tiles.append(a_tile)
+
+        def load_weights(w, name):
+            w_tile = held.tile([P, CB, C], BF16, name=name)
+            nc.sync.dma_start(w_tile[:], w.rearrange("(p k) m -> p k m", k=CB))
+            weights.append(w_tile)
+
+        load_act(0)
         tables = []
-        act_tiles = {}
         for b in range(CB):
             table = held.tile([P, S], F32, name="table%d" % b)
-            nc.sync.dma_start(table[:], obs_emb[b * P : (b + 1) * P, :])
+            nc.sync.dma_start(table[:], obs_blocks[b, :, :])
             tables.append(table)
-            act_tiles[(0, b)] = load_act(0, b)
-
-        weights = []
-        for i, w in enumerate((wq, wk, wv)):
-            w_tile = held.tile([P, CB, C], BF16, name="w%d" % i)
-            nc.sync.dma_start(w_tile[:], w.rearrange("(k p) m -> p k m", p=P))
-            weights.append(w_tile)
+        load_weights(wq, "wq_tile")
 
         type_sum = held.tile([P, CB], F32, name="type_sum")
         nc.vector.tensor_tensor(type_sum[:], t_act[:], t_obs[:], ADD)
@@ -86,56 +88,73 @@ def tile_transformerrope_b_kernel(
         nc.vector.memset(averager[:], 1.0 / C)
         eps = held.tile([P, 1], F32, name="eps")
         nc.vector.memset(eps[:], EPS)
+        warmed = held.tile([P, 1], F32, name="warmed")
+        nc.scalar.activation(warmed[:], eps[:], FUNC.Abs_reciprocal_sqrt)
 
+        x_rows = out[0:C, :].rearrange("(p a) n -> a p n", a=CB)
+        pair_tiles = {}
+        totals = {}
+        means = {}
+        rstds = {}
         h_tiles = {}
 
-        def prepare(piece):
+        def look_up(piece, blocks):
             piece_offsets = offsets[:, piece * OFFS_COLS : (piece + 1) * OFFS_COLS]
-            cols = slice(piece * PIECE, (piece + 1) * PIECE)
-            x_tiles = []
-            for b in range(CB):
-                a = act_tiles[(piece, b)]
-                nc.scalar.activation(a[:], a[:], FUNC.Identity, bias=type_sum[:, b : b + 1])
-                x = xs_pool.tile([P, PIECE], F32, name="x")
-                nc.vector.tensor_tensor(x[:], tables[b][:].indirect(piece_offsets), a[:], ADD)
-                x_tiles.append(x)
-                sq = squares.tile([P, PIECE], F32, name="sq")
-                nc.scalar.activation(sq[:], x[:], FUNC.Square)
+            gathered = {}
+            for b in blocks:
+                y = gathered_pool.tile([P, PIECE], F32, name="y")
+                nc.vector.tensor_tensor(
+                    y[:], tables[b][:].indirect(piece_offsets), act_tiles[piece][:, b, :], ADD
+                )
+                gathered[b] = y
+            for b in blocks:
+                pair = pairs.tile([P, 2 * PIECE], F32, name="pair")
+                types = type_sum[:, b : b + 1]
+                nc.scalar.activation(pair[:, 0:PIECE], gathered[b][:], FUNC.Identity, bias=types)
+                nc.scalar.activation(pair[:, PIECE:], gathered[b][:], FUNC.Square, bias=types)
+                nc.sync.dma_start(x_rows[b, :, piece_cols(piece)], pair[:, 0:PIECE])
+                pair_tiles[(piece, b)] = pair
+            for b in blocks:
                 if b == 0:
-                    run_x, run_sq = x, sq
+                    totals[piece] = pair_tiles[(piece, b)]
                 else:
-                    next_x = sums.tile([P, PIECE], F32, name="run_x")
-                    nc.vector.tensor_tensor(next_x[:], run_x[:], x[:], ADD)
-                    next_sq = sums.tile([P, PIECE], F32, name="run_sq")
-                    nc.vector.tensor_tensor(next_sq[:], run_sq[:], sq[:], ADD)
-                    run_x, run_sq = next_x, next_sq
+                    grown = sums.tile([P, 2 * PIECE], F32, name="total")
+                    nc.vector.tensor_tensor(
+                        grown[:], totals[piece][:], pair_tiles[(piece, b)][:], ADD
+                    )
+                    totals[piece] = grown
 
-            mean = moments.tile([P, PIECE], F32, name="mean")
-            nc.tensor.matmul(mean[:], averager[:], run_x[:], start=True, stop=True)
-            mean_sq = moments.tile([P, PIECE], F32, name="mean_sq")
-            nc.tensor.matmul(mean_sq[:], averager[:], run_sq[:], start=True, stop=True)
+        def moments(piece):
+            both = moments_pool.tile([P, 2 * PIECE], F32, name="both")
+            nc.tensor.matmul(both[:], averager[:], totals[piece][:], start=True, stop=True)
+            means[piece] = both[:, 0:PIECE]
             sq_mean = stats.tile([P, PIECE], F32, name="sq_mean")
-            nc.scalar.activation(sq_mean[:], mean[:], FUNC.Square)
+            nc.scalar.activation(sq_mean[:], both[:, 0:PIECE], FUNC.Square)
             var = stats.tile([P, PIECE], F32, name="var")
-            nc.vector.tensor_tensor(var[:], mean_sq[:], sq_mean[:], SUB)
+            nc.vector.tensor_tensor(var[:], both[:, PIECE:], sq_mean[:], SUB)
             rstd = stats.tile([P, PIECE], F32, name="rstd")
             nc.scalar.activation(rstd[:], var[:], FUNC.Abs_reciprocal_sqrt, bias=eps[:])
+            rstds[piece] = rstd
 
-            for b in range(CB):
+        def normalise(piece, blocks):
+            centred_tiles = {}
+            for b in blocks:
                 centred = centred_pool.tile([P, PIECE], F32, name="centred")
-                nc.vector.tensor_tensor(centred[:], x_tiles[b][:], mean[:], SUB)
-                nc.vector.tensor_tensor(centred[:], centred[:], rstd[:], MULT)
+                nc.vector.tensor_tensor(
+                    centred[:], pair_tiles[(piece, b)][:, 0:PIECE], means[piece], SUB
+                )
+                centred_tiles[b] = centred
+            for b in blocks:
+                centred = centred_tiles[b]
+                nc.vector.tensor_tensor(centred[:], centred[:], rstds[piece][:], MULT)
                 h = hs_pool.tile([P, PIECE], BF16, name="h")
                 nc.scalar.activation(
                     h[:], centred[:], FUNC.Identity,
                     bias=shift[:, b : b + 1], scale=gain[:, b : b + 1],
                 )
                 h_tiles[(piece, b)] = h
-            for b in range(CB):
-                nc.sync.dma_start(out[b * P : (b + 1) * P, cols], x_tiles[b][:])
 
-        def project(piece, group):
-            cols = slice(piece * PIECE, (piece + 1) * PIECE)
+        def accumulate(piece, group):
             blocks = range(group * GROUP, (group + 1) * GROUP)
             banks = [banks_pool.tile([P, PIECE], F32, name="bank") for m in blocks]
             for k in range(CB):
@@ -145,21 +164,40 @@ def tile_transformerrope_b_kernel(
                         bank[:], weights[m // CB][:, k, w_cols], h_tiles[(piece, k)][:],
                         start=(k == 0), stop=(k == CB - 1),
                     )
-            for m, bank in zip(blocks, banks):
-                staged = staging.tile([P, PIECE], F32, name="staged")
-                if m % GROUP == 1:
-                    nc.vector.tensor_scalar(staged[:], bank[:], bias[:, m : m + 1], None, ADD)
-                else:
-                    nc.scalar.activation(staged[:], bank[:], FUNC.Identity, bias=bias[:, m : m + 1])
-                nc.sync.dma_start(out[C + m * P : C + (m + 1) * P, cols], staged[:])
+            return banks
 
-        prepare(0)
-        for b in range(CB):
-            act_tiles[(1, b)] = load_act(1, b)
-        for group in range(GROUPS // 2):
-            project(0, group)
-        prepare(1)
-        for group in range(GROUPS // 2, GROUPS):
-            project(0, group)
-        for group in range(GROUPS):
-            project(1, group)
+        def empty(piece, group, banks):
+            staged = staging.tile([P, GROUP, PIECE], F32, name="staged")
+            for i, bank in enumerate(banks):
+                m = group * GROUP + i
+                nc.scalar.activation(
+                    staged[:, i, :], bank[:], FUNC.Identity, bias=bias[:, m : m + 1]
+                )
+            rows = slice(C + group * GROUP * P, C + (group + 1) * GROUP * P)
+            nc.sync.dma_start(
+                out[rows, piece_cols(piece)].rearrange("(i p) n -> p i n", p=P), staged[:]
+            )
+
+        for first in range(0, CB, SHARE):
+            look_up(0, range(first, first + SHARE))
+        load_act(1)
+        load_weights(wk, "wk_tile")
+        load_weights(wv, "wv_tile")
+        load_act(2)
+        load_act(3)
+        moments(0)
+        for first in range(0, CB, SHARE):
+            normalise(0, range(first, first + SHARE))
+        for piece in range(PIECES):
+            following = piece + 1
+            for group in range(GROUPS):
+                if following < PIECES and group == GROUPS // 2:
+                    moments(following)
+                banks = accumulate(piece, group)
+                if following < PIECES:
+                    first = (group % (GROUPS // 2)) * SHARE
+                    if group < GROUPS // 2:
+                        look_up(following, range(first, first + SHARE))
+                    else:
+                        normalise(following, range(first, first + SHARE))
+                empty(piece, group, banks)

@@ -20,7 +20,9 @@ OFFS_COLS = PIECE // 16
 MB = 3 * CB
 GROUP = 3
 GROUPS = MB // GROUP
-SHARE = CB // (GROUPS // 2)
+SHARE = 3
+SHARES = -(-CB // SHARE)
+NORM_FROM = GROUPS - SHARES
 
 FLOPS = 2 * 3 * C * C * N
 
@@ -37,7 +39,7 @@ def tile_transformerrope_b_kernel(
         tc.tile_pool(name="sums", bufs=3) as sums,
         tc.tile_pool(name="stats", bufs=1) as stats,
         tc.tile_pool(name="centred", bufs=CB) as centred_pool,
-        tc.tile_pool(name="staging", bufs=3) as staging,
+        tc.tile_pool(name="staging", bufs=6) as staging,
         tc.psum_pool(name="moments", bufs=2) as moments_pool,
         tc.psum_pool(name="banks", bufs=2 * GROUP) as banks_pool,
     ):
@@ -114,6 +116,8 @@ def tile_transformerrope_b_kernel(
                 nc.scalar.activation(pair[:, PIECE:], gathered[b][:], FUNC.Square, bias=types)
                 nc.sync.dma_start(x_rows[b, :, piece_cols(piece)], pair[:, 0:PIECE])
                 pair_tiles[(piece, b)] = pair
+
+        def add_up(piece, blocks):
             for b in blocks:
                 if b == 0:
                     totals[piece] = pair_tiles[(piece, b)]
@@ -124,9 +128,12 @@ def tile_transformerrope_b_kernel(
                     )
                     totals[piece] = grown
 
-        def moments(piece):
+        def moments(piece, parts):
             both = moments_pool.tile([P, 2 * PIECE], F32, name="both")
-            nc.tensor.matmul(both[:], averager[:], totals[piece][:], start=True, stop=True)
+            for i, part in enumerate(parts):
+                nc.tensor.matmul(
+                    both[:], averager[:], part[:], start=(i == 0), stop=(i == len(parts) - 1)
+                )
             means[piece] = both[:, 0:PIECE]
             sq_mean = stats.tile([P, PIECE], F32, name="sq_mean")
             nc.scalar.activation(sq_mean[:], both[:, 0:PIECE], FUNC.Square)
@@ -178,26 +185,27 @@ def tile_transformerrope_b_kernel(
                 out[rows, piece_cols(piece)].rearrange("(i p) n -> p i n", p=P), staged[:]
             )
 
-        for first in range(0, CB, SHARE):
-            look_up(0, range(first, first + SHARE))
+        for b in range(CB):
+            look_up(0, range(b, b + 1))
         load_act(1)
         load_weights(wk, "wk_tile")
         load_weights(wv, "wv_tile")
-        load_act(2)
-        load_act(3)
-        moments(0)
-        for first in range(0, CB, SHARE):
-            normalise(0, range(first, first + SHARE))
+        moments(0, [pair_tiles[(0, b)] for b in range(CB)])
+        normalise(0, range(CB))
+
+        def share(step):
+            return range(max(step * SHARE, 0), min((step + 1) * SHARE, CB))
+
         for piece in range(PIECES):
             following = piece + 1
             for group in range(GROUPS):
-                if following < PIECES and group == GROUPS // 2:
-                    moments(following)
+                if following < PIECES and group == NORM_FROM:
+                    moments(following, [totals[following]])
+                if following + 1 < PIECES and group == NORM_FROM:
+                    load_act(following + 1)
                 banks = accumulate(piece, group)
                 if following < PIECES:
-                    first = (group % (GROUPS // 2)) * SHARE
-                    if group < GROUPS // 2:
-                        look_up(following, range(first, first + SHARE))
-                    else:
-                        normalise(following, range(first, first + SHARE))
+                    look_up(following, share(group))
+                    add_up(following, share(group - 1))
+                    normalise(following, share(group - NORM_FROM))
                 empty(piece, group, banks)

@@ -17,9 +17,9 @@ CB = C // P
 PIECE = 256
 PIECES = N // PIECE
 OFFS_COLS = PIECE // 16
-MB = 3 * CB
+ROW_BLOCKS = 3 * C // P
 GROUP = 3
-GROUPS = MB // GROUP
+GROUPS = ROW_BLOCKS // GROUP
 SHARE = 3
 SHARES = -(-CB // SHARE)
 NORM_FROM = GROUPS - SHARES
@@ -37,8 +37,9 @@ def tile_transformerrope_b_kernel(
         tc.tile_pool(name="pairs", bufs=2 * CB) as pairs,
         tc.tile_pool(name="hs", bufs=2 * CB) as hs_pool,
         tc.tile_pool(name="sums", bufs=3) as sums,
+        tc.tile_pool(name="halves", bufs=1) as halves,
         tc.tile_pool(name="stats", bufs=1) as stats,
-        tc.tile_pool(name="centred", bufs=CB) as centred_pool,
+        tc.tile_pool(name="centred", bufs=2 * SHARE) as centred_pool,
         tc.tile_pool(name="staging", bufs=6) as staging,
         tc.psum_pool(name="moments", bufs=2) as moments_pool,
         tc.psum_pool(name="banks", bufs=2 * GROUP) as banks_pool,
@@ -52,17 +53,17 @@ def tile_transformerrope_b_kernel(
         channel_vectors = []
         for i, vec in enumerate((type_act, type_obs, ln_g, ln_b)):
             v_tile = held.tile([P, CB], F32, name="vec%d" % i)
-            nc.scalar.dma_start(v_tile[:], vec.rearrange("(p a) o -> p (a o)", a=CB))
+            nc.scalar.dma_start(v_tile[:], vec.rearrange("(p b) o -> p (b o)", b=CB))
             channel_vectors.append(v_tile)
         t_act, t_obs, gain, shift = channel_vectors
-        bias = held.tile([P, MB], F32, name="bias")
+        bias = held.tile([P, ROW_BLOCKS], F32, name="bias")
         for i, vec in enumerate((bq, bk, bv)):
             nc.scalar.dma_start(
-                bias[:, i * CB : (i + 1) * CB], vec.rearrange("(a p) o -> p (a o)", p=P)
+                bias[:, i * CB : (i + 1) * CB], vec.rearrange("(m p) o -> p (m o)", p=P)
             )
 
-        act_blocks = act.rearrange("(p a) n -> p a n", a=CB)
-        obs_blocks = obs_emb.rearrange("(p a) s -> a p s", a=CB)
+        act_blocks = act.rearrange("(p b) n -> p b n", b=CB)
+        obs_blocks = obs_emb.rearrange("(p b) s -> b p s", b=CB)
         act_tiles = []
         weights = []
 
@@ -73,7 +74,7 @@ def tile_transformerrope_b_kernel(
 
         def load_weights(w, name):
             w_tile = held.tile([P, CB, C], BF16, name=name)
-            nc.sync.dma_start(w_tile[:], w.rearrange("(p k) m -> p k m", k=CB))
+            nc.sync.dma_start(w_tile[:], w.rearrange("(p b) m -> p b m", b=CB))
             weights.append(w_tile)
 
         load_act(0)
@@ -86,16 +87,19 @@ def tile_transformerrope_b_kernel(
 
         type_sum = held.tile([P, CB], F32, name="type_sum")
         nc.vector.tensor_tensor(type_sum[:], t_act[:], t_obs[:], ADD)
-        averager = held.tile([P, P], F32, name="averager")
-        nc.vector.memset(averager[:], 1.0 / C)
+        averaging = held.tile([P, P], F32, name="averaging")
+        nc.vector.memset(averaging[:], 1.0 / C)
+        averaging_bf = held.tile([P, P], BF16, name="averaging_bf")
+        nc.vector.memset(averaging_bf[:], 1.0 / C)
         eps = held.tile([P, 1], F32, name="eps")
         nc.vector.memset(eps[:], EPS)
         warmed = held.tile([P, 1], F32, name="warmed")
         nc.scalar.activation(warmed[:], eps[:], FUNC.Abs_reciprocal_sqrt)
 
-        x_rows = out[0:C, :].rearrange("(p a) n -> a p n", a=CB)
+        x_rows = out[0:C, :].rearrange("(p b) n -> b p n", b=CB)
         pair_tiles = {}
         totals = {}
+        split_totals = {}
         means = {}
         rstds = {}
         h_tiles = {}
@@ -127,12 +131,19 @@ def tile_transformerrope_b_kernel(
                         grown[:], totals[piece][:], pair_tiles[(piece, b)][:], ADD
                     )
                     totals[piece] = grown
+            if CB - 1 in blocks:
+                coarse = halves.tile([P, 2 * PIECE], BF16, name="coarse")
+                nc.scalar.copy(coarse[:], totals[piece][:])
+                fine = halves.tile([P, 2 * PIECE], BF16, name="fine")
+                nc.vector.tensor_tensor(fine[:], totals[piece][:], coarse[:], SUB)
+                split_totals[piece] = [coarse, fine]
 
-        def moments(piece, parts):
+        def moments(piece, averaging_matrix, parts):
             both = moments_pool.tile([P, 2 * PIECE], F32, name="both")
             for i, part in enumerate(parts):
                 nc.tensor.matmul(
-                    both[:], averager[:], part[:], start=(i == 0), stop=(i == len(parts) - 1)
+                    both[:], averaging_matrix[:], part[:],
+                    start=(i == 0), stop=(i == len(parts) - 1),
                 )
             means[piece] = both[:, 0:PIECE]
             sq_mean = stats.tile([P, PIECE], F32, name="sq_mean")
@@ -162,14 +173,14 @@ def tile_transformerrope_b_kernel(
                 h_tiles[(piece, b)] = h
 
         def accumulate(piece, group):
-            blocks = range(group * GROUP, (group + 1) * GROUP)
-            banks = [banks_pool.tile([P, PIECE], F32, name="bank") for m in blocks]
-            for k in range(CB):
-                for m, bank in zip(blocks, banks):
+            row_blocks = range(group * GROUP, (group + 1) * GROUP)
+            banks = [banks_pool.tile([P, PIECE], F32, name="bank") for m in row_blocks]
+            for b in range(CB):
+                for m, bank in zip(row_blocks, banks):
                     w_cols = slice((m % CB) * P, (m % CB + 1) * P)
                     nc.tensor.matmul(
-                        bank[:], weights[m // CB][:, k, w_cols], h_tiles[(piece, k)][:],
-                        start=(k == 0), stop=(k == CB - 1),
+                        bank[:], weights[m // CB][:, b, w_cols], h_tiles[(piece, b)][:],
+                        start=(b == 0), stop=(b == CB - 1),
                     )
             return banks
 
@@ -185,22 +196,23 @@ def tile_transformerrope_b_kernel(
                 out[rows, piece_cols(piece)].rearrange("(i p) n -> p i n", p=P), staged[:]
             )
 
+        def share(step):
+            return range(max(step * SHARE, 0), min((step + 1) * SHARE, CB))
+
         for b in range(CB):
             look_up(0, range(b, b + 1))
         load_act(1)
         load_weights(wk, "wk_tile")
         load_weights(wv, "wv_tile")
-        moments(0, [pair_tiles[(0, b)] for b in range(CB)])
-        normalise(0, range(CB))
-
-        def share(step):
-            return range(max(step * SHARE, 0), min((step + 1) * SHARE, CB))
+        moments(0, averaging, [pair_tiles[(0, b)] for b in range(CB)])
+        for step in range(SHARES):
+            normalise(0, share(step))
 
         for piece in range(PIECES):
             following = piece + 1
             for group in range(GROUPS):
                 if following < PIECES and group == NORM_FROM:
-                    moments(following, [totals[following]])
+                    moments(following, averaging_bf, split_totals[following])
                 if following + 1 < PIECES and group == NORM_FROM:
                     load_act(following + 1)
                 banks = accumulate(piece, group)

@@ -1,4 +1,5 @@
 import concourse.mybir as mybir
+from concourse.masks import make_identity
 
 F32 = mybir.dt.float32
 BF16 = mybir.dt.bfloat16
@@ -20,6 +21,7 @@ OFFS_COLS = PIECE // 16
 ROW_BLOCKS = 3 * C // P
 GROUP = 3
 GROUPS = ROW_BLOCKS // GROUP
+BIAS_ROWS = 64
 SHARE = 3
 SHARES = -(-CB // SHARE)
 NORM_FROM = GROUPS - SHARES
@@ -56,11 +58,18 @@ def tile_transformerrope_b_kernel(
             nc.scalar.dma_start(v_tile[:], vec.rearrange("(p b) o -> p (b o)", b=CB))
             channel_vectors.append(v_tile)
         t_act, t_obs, gain, shift = channel_vectors
-        bias = held.tile([P, ROW_BLOCKS], F32, name="bias")
+        bias_rows = held.tile([BIAS_ROWS, P], F32, name="bias_rows")
+        nc.vector.memset(bias_rows[:], 0.0)
         for i, vec in enumerate((bq, bk, bv)):
             nc.scalar.dma_start(
-                bias[:, i * CB : (i + 1) * CB], vec.rearrange("(m p) o -> p (m o)", p=P)
+                bias_rows[i * CB : (i + 1) * CB, :], vec.rearrange("(m p) o -> m (p o)", p=P)
             )
+        identity = held.tile([BIAS_ROWS, BIAS_ROWS], F32, name="identity")
+        make_identity(nc, identity[:])
+        bias_columns = moments_pool.tile([P, BIAS_ROWS], F32, name="bias_columns", tag="both")
+        nc.tensor.transpose(bias_columns[:], bias_rows[:], identity[:])
+        bias = held.tile([P, BIAS_ROWS], F32, name="bias")
+        nc.vector.tensor_copy(bias[:], bias_columns[:])
 
         act_blocks = act.rearrange("(p b) n -> p b n", b=CB)
         obs_blocks = obs_emb.rearrange("(p b) s -> b p s", b=CB)

@@ -20,11 +20,11 @@ PIECES = N // PIECE
 OFFS_COLS = PIECE // 16
 ROW_BLOCKS = 3 * C // P
 GROUP = 3
-GROUPS = ROW_BLOCKS // GROUP
+FIRST_GROUP = 6
 BIAS_ROWS = 64
 SHARE = 3
 SHARES = -(-CB // SHARE)
-NORM_FROM = GROUPS - SHARES
+PSUM_BANKS = 8
 
 FLOPS = 2 * 3 * C * C * N
 
@@ -42,9 +42,8 @@ def tile_transformerrope_b_kernel(
         tc.tile_pool(name="halves", bufs=1) as halves,
         tc.tile_pool(name="stats", bufs=1) as stats,
         tc.tile_pool(name="centred", bufs=2 * SHARE) as centred_pool,
-        tc.tile_pool(name="staging", bufs=6) as staging,
-        tc.psum_pool(name="moments", bufs=2) as moments_pool,
-        tc.psum_pool(name="banks", bufs=2 * GROUP) as banks_pool,
+        tc.tile_pool(name="staging", bufs=18) as staging,
+        tc.psum_pool(name="psum", bufs=PSUM_BANKS) as psum,
     ):
         def piece_cols(piece):
             return slice(piece * PIECE, (piece + 1) * PIECE)
@@ -66,7 +65,7 @@ def tile_transformerrope_b_kernel(
             )
         identity = held.tile([BIAS_ROWS, BIAS_ROWS], F32, name="identity")
         make_identity(nc, identity[:])
-        bias_columns = moments_pool.tile([P, BIAS_ROWS], F32, name="bias_columns", tag="both")
+        bias_columns = psum.tile([P, BIAS_ROWS], F32, name="bias_columns", tag="bank")
         nc.tensor.transpose(bias_columns[:], bias_rows[:], identity[:])
         bias = held.tile([P, BIAS_ROWS], F32, name="bias")
         nc.vector.tensor_copy(bias[:], bias_columns[:])
@@ -148,7 +147,7 @@ def tile_transformerrope_b_kernel(
                 split_totals[piece] = [coarse, fine]
 
         def moments(piece, averaging_matrix, parts):
-            both = moments_pool.tile([P, 2 * PIECE], F32, name="both")
+            both = psum.tile([P, 2 * PIECE], F32, name="both", tag="bank")
             for i, part in enumerate(parts):
                 nc.tensor.matmul(
                     both[:], averaging_matrix[:], part[:],
@@ -181,29 +180,29 @@ def tile_transformerrope_b_kernel(
                 )
                 h_tiles[(piece, b)] = h
 
-        def accumulate(piece, group):
-            row_blocks = range(group * GROUP, (group + 1) * GROUP)
-            banks = [banks_pool.tile([P, PIECE], F32, name="bank") for m in row_blocks]
-            for b in range(CB):
-                for m, bank in zip(row_blocks, banks):
-                    w_cols = slice((m % CB) * P, (m % CB + 1) * P)
-                    nc.tensor.matmul(
-                        bank[:], weights[m // CB][:, b, w_cols], h_tiles[(piece, b)][:],
-                        start=(b == 0), stop=(b == CB - 1),
-                    )
+        def accumulate(piece, row_blocks, side_by_side):
+            banks = {m: psum.tile([P, PIECE], F32, name="bank", tag="bank") for m in row_blocks}
+            if side_by_side:
+                order = [(m, b) for b in range(CB) for m in row_blocks]
+            else:
+                order = [(m, b) for m in row_blocks for b in range(CB)]
+            for m, b in order:
+                w_cols = slice((m % CB) * P, (m % CB + 1) * P)
+                nc.tensor.matmul(
+                    banks[m][:], weights[m // CB][:, b, w_cols], h_tiles[(piece, b)][:],
+                    start=(b == 0), stop=(b == CB - 1),
+                )
             return banks
 
-        def empty(piece, group, banks):
-            staged = staging.tile([P, GROUP, PIECE], F32, name="staged")
-            for i, bank in enumerate(banks):
-                m = group * GROUP + i
-                nc.scalar.activation(
-                    staged[:, i, :], bank[:], FUNC.Identity, bias=bias[:, m : m + 1]
-                )
-            rows = slice(C + group * GROUP * P, C + (group + 1) * GROUP * P)
-            nc.sync.dma_start(
-                out[rows, piece_cols(piece)].rearrange("(i p) n -> p i n", p=P), staged[:]
-            )
+        def empty(piece, row_blocks, banks):
+            for m in row_blocks:
+                staged = staging.tile([P, PIECE], F32, name="staged")
+                nc.scalar.activation(staged[:], banks[m][:], FUNC.Identity, bias=bias[:, m : m + 1])
+                nc.sync.dma_start(out[C + m * P : C + (m + 1) * P, piece_cols(piece)], staged[:])
+
+        def groups_of(piece):
+            first = FIRST_GROUP if piece == 0 else GROUP
+            return [range(0, first)] + [range(m, m + GROUP) for m in range(first, ROW_BLOCKS, GROUP)]
 
         def share(step):
             return range(max(step * SHARE, 0), min((step + 1) * SHARE, CB))
@@ -219,14 +218,16 @@ def tile_transformerrope_b_kernel(
 
         for piece in range(PIECES):
             following = piece + 1
-            for group in range(GROUPS):
-                if following < PIECES and group == NORM_FROM:
+            groups = groups_of(piece)
+            norm_from = len(groups) - SHARES
+            for step, row_blocks in enumerate(groups):
+                if following < PIECES and step == norm_from:
                     moments(following, averaging_bf, split_totals[following])
-                if following + 1 < PIECES and group == NORM_FROM:
+                if following + 1 < PIECES and step == norm_from:
                     load_act(following + 1)
-                banks = accumulate(piece, group)
+                banks = accumulate(piece, row_blocks, side_by_side=(piece == 0 and step == 0))
                 if following < PIECES:
-                    look_up(following, share(group))
-                    add_up(following, share(group - 1))
-                    normalise(following, share(group - NORM_FROM))
-                empty(piece, group, banks)
+                    look_up(following, share(step))
+                    add_up(following, share(step - 1))
+                    normalise(following, share(step - norm_from))
+                empty(piece, row_blocks, banks)

@@ -17,14 +17,17 @@ EPS = 1e-5
 CB = C // P
 PIECE = 256
 PIECES = N // PIECE
-OFFS_COLS = PIECE // 16
+WHOLE = (0, PIECE)
+HEAD = 64
 ROW_BLOCKS = 3 * C // P
 GROUP = 3
 FIRST_GROUP = 6
 BIAS_ROWS = 64
 SHARE = 3
 SHARES = -(-CB // SHARE)
+NORM_FROM = 5
 PSUM_BANKS = 8
+HALF_CB = CB // 2
 
 FLOPS = 2 * 3 * C * C * N
 
@@ -35,12 +38,11 @@ def tile_transformerrope_b_kernel(
     nc = tc.nc
     with (
         tc.tile_pool(name="held", bufs=1) as held,
-        tc.tile_pool(name="gathered", bufs=2 * SHARE) as gathered_pool,
         tc.tile_pool(name="pairs", bufs=2 * CB) as pairs,
         tc.tile_pool(name="hs", bufs=2 * CB) as hs_pool,
         tc.tile_pool(name="sums", bufs=3) as sums,
         tc.tile_pool(name="halves", bufs=1) as halves,
-        tc.tile_pool(name="stats", bufs=1) as stats,
+        tc.tile_pool(name="stats", bufs=2) as stats,
         tc.tile_pool(name="centred", bufs=2 * SHARE) as centred_pool,
         tc.tile_pool(name="staging", bufs=18) as staging,
         tc.psum_pool(name="psum", bufs=PSUM_BANKS) as psum,
@@ -81,9 +83,13 @@ def tile_transformerrope_b_kernel(
             act_tiles.append(a_tile)
 
         def load_weights(w, name):
-            w_tile = held.tile([P, CB, C], BF16, name=name)
-            nc.sync.dma_start(w_tile[:], w.rearrange("(p b) m -> p b m", b=CB))
-            weights.append(w_tile)
+            w_blocks = w.rearrange("(p b) m -> p b m", b=CB)
+            halves_of_w = []
+            for half in range(2):
+                w_tile = held.tile([P, HALF_CB, C], BF16, name="%s%d" % (name, half))
+                nc.sync.dma_start(w_tile[:], w_blocks[:, half * HALF_CB : (half + 1) * HALF_CB, :])
+                halves_of_w.append(w_tile)
+            weights.append(halves_of_w)
 
         load_act(0)
         tables = []
@@ -109,25 +115,34 @@ def tile_transformerrope_b_kernel(
         totals = {}
         split_totals = {}
         means = {}
+        mean_sqs = {}
         rstds = {}
         h_tiles = {}
 
-        def look_up(piece, blocks):
-            piece_offsets = offsets[:, piece * OFFS_COLS : (piece + 1) * OFFS_COLS]
-            gathered = {}
+        def spans_of(piece):
+            return [(0, HEAD), (HEAD, PIECE)] if piece == 0 else [WHOLE]
+
+        def look_up(piece, span, blocks):
+            lo, hi = span
+            first_token = piece * PIECE + lo
+            span_offsets = offsets[:, first_token // 16 : (first_token + hi - lo) // 16]
             for b in blocks:
-                y = gathered_pool.tile([P, PIECE], F32, name="y")
-                nc.vector.tensor_tensor(
-                    y[:], tables[b][:].indirect(piece_offsets), act_tiles[piece][:, b, :], ADD
+                nc.vector.tensor_scalar_add(
+                    act_tiles[piece][:, b, lo:hi], act_tiles[piece][:, b, lo:hi],
+                    type_sum[:, b : b + 1],
                 )
-                gathered[b] = y
             for b in blocks:
-                pair = pairs.tile([P, 2 * PIECE], F32, name="pair")
-                types = type_sum[:, b : b + 1]
-                nc.scalar.activation(pair[:, 0:PIECE], gathered[b][:], FUNC.Identity, bias=types)
-                nc.scalar.activation(pair[:, PIECE:], gathered[b][:], FUNC.Square, bias=types)
-                nc.sync.dma_start(x_rows[b, :, piece_cols(piece)], pair[:, 0:PIECE])
-                pair_tiles[(piece, b)] = pair
+                if lo == 0:
+                    pair_tiles[(piece, b)] = pairs.tile([P, 2 * PIECE], F32, name="pair")
+                nc.vector.tensor_tensor(
+                    pair_tiles[(piece, b)][:, lo:hi], tables[b][:].indirect(span_offsets),
+                    act_tiles[piece][:, b, lo:hi], ADD,
+                )
+            for b in blocks:
+                pair = pair_tiles[(piece, b)]
+                nc.scalar.activation(pair[:, PIECE + lo : PIECE + hi], pair[:, lo:hi], FUNC.Square)
+                if hi == PIECE:
+                    nc.sync.dma_start(x_rows[b, :, piece_cols(piece)], pair[:, 0:PIECE])
 
         def add_up(piece, blocks):
             for b in blocks:
@@ -146,53 +161,57 @@ def tile_transformerrope_b_kernel(
                 nc.vector.tensor_tensor(fine[:], totals[piece][:], coarse[:], SUB)
                 split_totals[piece] = [coarse, fine]
 
-        def moments(piece, averaging_matrix, parts):
-            both = psum.tile([P, 2 * PIECE], F32, name="both", tag="bank")
-            for i, part in enumerate(parts):
+        def average(piece, span, averaging_matrix, part, first, last):
+            lo, hi = span
+            if first:
+                means[(piece, span)] = psum.tile([P, hi - lo], F32, name="mean", tag="bank")
+                mean_sqs[(piece, span)] = psum.tile([P, hi - lo], F32, name="mean_sq", tag="bank")
+            for bank, at in ((means[(piece, span)], 0), (mean_sqs[(piece, span)], PIECE)):
                 nc.tensor.matmul(
-                    both[:], averaging_matrix[:], part[:],
-                    start=(i == 0), stop=(i == len(parts) - 1),
+                    bank[:], averaging_matrix[:], part[:, at + lo : at + hi], start=first, stop=last
                 )
-            means[piece] = both[:, 0:PIECE]
-            sq_mean = stats.tile([P, PIECE], F32, name="sq_mean")
-            nc.scalar.activation(sq_mean[:], both[:, 0:PIECE], FUNC.Square)
-            var = stats.tile([P, PIECE], F32, name="var")
-            nc.vector.tensor_tensor(var[:], both[:, PIECE:], sq_mean[:], SUB)
-            rstd = stats.tile([P, PIECE], F32, name="rstd")
-            nc.scalar.activation(rstd[:], var[:], FUNC.Abs_reciprocal_sqrt, bias=eps[:])
-            rstds[piece] = rstd
 
-        def normalise(piece, blocks):
+        def deviation(piece, span):
+            width = span[1] - span[0]
+            sq_mean = stats.tile([P, width], F32, name="sq_mean")
+            nc.scalar.activation(sq_mean[:], means[(piece, span)][:], FUNC.Square)
+            var = stats.tile([P, width], F32, name="var")
+            nc.vector.tensor_tensor(var[:], mean_sqs[(piece, span)][:], sq_mean[:], SUB)
+            rstd = stats.tile([P, width], F32, name="rstd")
+            nc.scalar.activation(rstd[:], var[:], FUNC.Abs_reciprocal_sqrt, bias=eps[:])
+            rstds[(piece, span)] = rstd
+
+        def normalise(piece, span, blocks):
+            lo, hi = span
             centred_tiles = {}
             for b in blocks:
-                centred = centred_pool.tile([P, PIECE], F32, name="centred")
+                centred = centred_pool.tile([P, hi - lo], F32, name="centred")
                 nc.vector.tensor_tensor(
-                    centred[:], pair_tiles[(piece, b)][:, 0:PIECE], means[piece], SUB
+                    centred[:], pair_tiles[(piece, b)][:, lo:hi], means[(piece, span)][:], SUB
                 )
                 centred_tiles[b] = centred
             for b in blocks:
                 centred = centred_tiles[b]
-                nc.vector.tensor_tensor(centred[:], centred[:], rstds[piece][:], MULT)
-                h = hs_pool.tile([P, PIECE], BF16, name="h")
+                nc.vector.tensor_tensor(centred[:], centred[:], rstds[(piece, span)][:], MULT)
+                if lo == 0:
+                    h_tiles[(piece, b)] = hs_pool.tile([P, PIECE], BF16, name="h")
                 nc.scalar.activation(
-                    h[:], centred[:], FUNC.Identity,
+                    h_tiles[(piece, b)][:, lo:hi], centred[:], FUNC.Identity,
                     bias=shift[:, b : b + 1], scale=gain[:, b : b + 1],
                 )
-                h_tiles[(piece, b)] = h
 
-        def accumulate(piece, row_blocks, side_by_side):
-            banks = {m: psum.tile([P, PIECE], F32, name="bank", tag="bank") for m in row_blocks}
+        def accumulate(piece, span, row_blocks, banks, side_by_side):
+            lo, hi = span
             if side_by_side:
                 order = [(m, b) for b in range(CB) for m in row_blocks]
             else:
                 order = [(m, b) for m in row_blocks for b in range(CB)]
             for m, b in order:
-                w_cols = slice((m % CB) * P, (m % CB + 1) * P)
+                w_tile = weights[m // CB][b // HALF_CB]
                 nc.tensor.matmul(
-                    banks[m][:], weights[m // CB][:, b, w_cols], h_tiles[(piece, b)][:],
-                    start=(b == 0), stop=(b == CB - 1),
+                    banks[m][:, lo:hi], w_tile[:, b % HALF_CB, (m % CB) * P : (m % CB + 1) * P],
+                    h_tiles[(piece, b)][:, lo:hi], start=(b == 0), stop=(b == CB - 1),
                 )
-            return banks
 
         def empty(piece, row_blocks, banks):
             for m in row_blocks:
@@ -208,26 +227,35 @@ def tile_transformerrope_b_kernel(
             return range(max(step * SHARE, 0), min((step + 1) * SHARE, CB))
 
         for b in range(CB):
-            look_up(0, range(b, b + 1))
+            for span in spans_of(0):
+                look_up(0, span, range(b, b + 1))
+                average(0, span, averaging, pair_tiles[(0, b)], first=(b == 0), last=(b == CB - 1))
         load_act(1)
         load_weights(wk, "wk_tile")
         load_weights(wv, "wv_tile")
-        moments(0, averaging, [pair_tiles[(0, b)] for b in range(CB)])
-        for step in range(SHARES):
-            normalise(0, share(step))
+        for span in spans_of(0):
+            deviation(0, span)
+            for step in range(SHARES):
+                normalise(0, span, share(step))
 
         for piece in range(PIECES):
             following = piece + 1
             groups = groups_of(piece)
-            norm_from = len(groups) - SHARES
             for step, row_blocks in enumerate(groups):
-                if following < PIECES and step == norm_from:
-                    moments(following, averaging_bf, split_totals[following])
-                if following + 1 < PIECES and step == norm_from:
+                if following < PIECES and step == NORM_FROM:
+                    for i, part in enumerate(split_totals[following]):
+                        average(following, WHOLE, averaging_bf, part, first=(i == 0), last=(i == 1))
+                    deviation(following, WHOLE)
+                if following + 1 < PIECES and step == NORM_FROM:
                     load_act(following + 1)
-                banks = accumulate(piece, row_blocks, side_by_side=(piece == 0 and step == 0))
+                banks = {m: psum.tile([P, PIECE], F32, name="bank", tag="bank") for m in row_blocks}
+                for span in spans_of(piece) if step == 0 else [WHOLE]:
+                    accumulate(piece, span, row_blocks, banks, side_by_side=(step == 0))
                 if following < PIECES:
-                    look_up(following, share(step))
+                    look_up(following, WHOLE, share(step))
                     add_up(following, share(step - 1))
-                    normalise(following, share(step - norm_from))
+                    normalise(following, WHOLE, share(step - NORM_FROM))
+                    if step == len(groups) - 1:
+                        for late in range(len(groups), NORM_FROM + SHARES):
+                            normalise(following, WHOLE, share(late - NORM_FROM))
                 empty(piece, row_blocks, banks)

@@ -18,7 +18,7 @@ CB = C // P
 PIECE = 256
 PIECES = N // PIECE
 WHOLE = (0, PIECE)
-HEAD = 64
+HEAD = 128
 ROW_BLOCKS = 3 * C // P
 GROUP = 3
 FIRST_GROUP = 6

@@ -79,7 +79,9 @@ def tile_transformerrope_b_kernel(
 
         def load_act(piece):
             a_tile = held.tile([P, CB, PIECE], F32, name="act%d" % piece)
-            nc.sync.dma_start(a_tile[:], act_blocks[:, :, piece_cols(piece)])
+            for half in range(2):
+                blocks = slice(half * HALF_CB, (half + 1) * HALF_CB)
+                nc.sync.dma_start(a_tile[:, blocks, :], act_blocks[:, blocks, piece_cols(piece)])
             act_tiles.append(a_tile)
 
         def load_weights(w, name):

import concourse.mybir as mybir
from concourse.masks import make_identity

F32 = mybir.dt.float32
BF16 = mybir.dt.bfloat16
U16 = mybir.dt.uint16
ADD = mybir.AluOpType.add
SUB = mybir.AluOpType.subtract
MULT = mybir.AluOpType.mult
FUNC = mybir.ActivationFunctionType

P = 128
C = 1024
S = 2048
N = 1024
EPS = 1e-5
CB = C // P
PIECE = 256
PIECES = N // PIECE
WHOLE = (0, PIECE)
HEAD = 128
ROW_BLOCKS = 3 * C // P
GROUP = 3
FIRST_GROUP = 6
BIAS_ROWS = 64
SHARE = 3
SHARES = -(-CB // SHARE)
NORM_FROM = 5
PSUM_BANKS = 8
HALF_CB = CB // 2

FLOPS = 2 * 3 * C * C * N


def tile_transformerrope_b_kernel(
    tc, obs_emb, act, type_act, type_obs, ln_g, ln_b, wq, bq, wk, bk, wv, bv, offs, out
):
    nc = tc.nc
    with (
        tc.tile_pool(name="held", bufs=1) as held,
        tc.tile_pool(name="pairs", bufs=2 * CB) as pairs,
        tc.tile_pool(name="hs", bufs=2 * CB) as hs_pool,
        tc.tile_pool(name="sums", bufs=3) as sums,
        tc.tile_pool(name="halves", bufs=1) as halves,
        tc.tile_pool(name="stats", bufs=2) as stats,
        tc.tile_pool(name="centred", bufs=2 * SHARE) as centred_pool,
        tc.tile_pool(name="staging", bufs=18) as staging,
        tc.psum_pool(name="psum", bufs=PSUM_BANKS) as psum,
    ):
        def piece_cols(piece):
            return slice(piece * PIECE, (piece + 1) * PIECE)

        offsets = held.tile([P, N // 16], U16, name="offsets")
        nc.sync.dma_start(offsets[:], offs)

        channel_vectors = []
        for i, vec in enumerate((type_act, type_obs, ln_g, ln_b)):
            v_tile = held.tile([P, CB], F32, name="vec%d" % i)
            nc.scalar.dma_start(v_tile[:], vec.rearrange("(p b) o -> p (b o)", b=CB))
            channel_vectors.append(v_tile)
        t_act, t_obs, gain, shift = channel_vectors
        bias_rows = held.tile([BIAS_ROWS, P], F32, name="bias_rows")
        nc.vector.memset(bias_rows[:], 0.0)
        for i, vec in enumerate((bq, bk, bv)):
            nc.scalar.dma_start(
                bias_rows[i * CB : (i + 1) * CB, :], vec.rearrange("(m p) o -> m (p o)", p=P)
            )
        identity = held.tile([BIAS_ROWS, BIAS_ROWS], F32, name="identity")
        make_identity(nc, identity[:])
        bias_columns = psum.tile([P, BIAS_ROWS], F32, name="bias_columns", tag="bank")
        nc.tensor.transpose(bias_columns[:], bias_rows[:], identity[:])
        bias = held.tile([P, BIAS_ROWS], F32, name="bias")
        nc.vector.tensor_copy(bias[:], bias_columns[:])

        act_blocks = act.rearrange("(p b) n -> p b n", b=CB)
        obs_blocks = obs_emb.rearrange("(p b) s -> b p s", b=CB)
        act_tiles = []
        weights = []

        def load_act(piece):
            a_tile = held.tile([P, CB, PIECE], F32, name="act%d" % piece)
            for half in range(2):
                blocks = slice(half * HALF_CB, (half + 1) * HALF_CB)
                nc.sync.dma_start(a_tile[:, blocks, :], act_blocks[:, blocks, piece_cols(piece)])
            act_tiles.append(a_tile)

        def load_weights(w, name):
            w_blocks = w.rearrange("(p b) m -> p b m", b=CB)
            halves_of_w = []
            for half in range(2):
                w_tile = held.tile([P, HALF_CB, C], BF16, name="%s%d" % (name, half))
                nc.sync.dma_start(w_tile[:], w_blocks[:, half * HALF_CB : (half + 1) * HALF_CB, :])
                halves_of_w.append(w_tile)
            weights.append(halves_of_w)

        load_act(0)
        tables = []
        for b in range(CB):
            table = held.tile([P, S], F32, name="table%d" % b)
            nc.sync.dma_start(table[:], obs_blocks[b, :, :])
            tables.append(table)
        load_weights(wq, "wq_tile")

        type_sum = held.tile([P, CB], F32, name="type_sum")
        nc.vector.tensor_tensor(type_sum[:], t_act[:], t_obs[:], ADD)
        averaging = held.tile([P, P], F32, name="averaging")
        nc.vector.memset(averaging[:], 1.0 / C)
        averaging_bf = held.tile([P, P], BF16, name="averaging_bf")
        nc.vector.memset(averaging_bf[:], 1.0 / C)
        eps = held.tile([P, 1], F32, name="eps")
        nc.vector.memset(eps[:], EPS)
        warmed = held.tile([P, 1], F32, name="warmed")
        nc.scalar.activation(warmed[:], eps[:], FUNC.Abs_reciprocal_sqrt)

        x_rows = out[0:C, :].rearrange("(p b) n -> b p n", b=CB)
        pair_tiles = {}
        totals = {}
        split_totals = {}
        means = {}
        mean_sqs = {}
        rstds = {}
        h_tiles = {}

        def spans_of(piece):
            return [(0, HEAD), (HEAD, PIECE)] if piece == 0 else [WHOLE]

        def look_up(piece, span, blocks):
            lo, hi = span
            first_token = piece * PIECE + lo
            span_offsets = offsets[:, first_token // 16 : (first_token + hi - lo) // 16]
            for b in blocks:
                nc.vector.tensor_scalar_add(
                    act_tiles[piece][:, b, lo:hi], act_tiles[piece][:, b, lo:hi],
                    type_sum[:, b : b + 1],
                )
            for b in blocks:
                if lo == 0:
                    pair_tiles[(piece, b)] = pairs.tile([P, 2 * PIECE], F32, name="pair")
                nc.vector.tensor_tensor(
                    pair_tiles[(piece, b)][:, lo:hi], tables[b][:].indirect(span_offsets),
                    act_tiles[piece][:, b, lo:hi], ADD,
                )
            for b in blocks:
                pair = pair_tiles[(piece, b)]
                nc.scalar.activation(pair[:, PIECE + lo : PIECE + hi], pair[:, lo:hi], FUNC.Square)
                if hi == PIECE:
                    nc.sync.dma_start(x_rows[b, :, piece_cols(piece)], pair[:, 0:PIECE])

        def add_up(piece, blocks):
            for b in blocks:
                if b == 0:
                    totals[piece] = pair_tiles[(piece, b)]
                else:
                    grown = sums.tile([P, 2 * PIECE], F32, name="total")
                    nc.vector.tensor_tensor(
                        grown[:], totals[piece][:], pair_tiles[(piece, b)][:], ADD
                    )
                    totals[piece] = grown
            if CB - 1 in blocks:
                coarse = halves.tile([P, 2 * PIECE], BF16, name="coarse")
                nc.scalar.copy(coarse[:], totals[piece][:])
                fine = halves.tile([P, 2 * PIECE], BF16, name="fine")
                nc.vector.tensor_tensor(fine[:], totals[piece][:], coarse[:], SUB)
                split_totals[piece] = [coarse, fine]

        def average(piece, span, averaging_matrix, part, first, last):
            lo, hi = span
            if first:
                means[(piece, span)] = psum.tile([P, hi - lo], F32, name="mean", tag="bank")
                mean_sqs[(piece, span)] = psum.tile([P, hi - lo], F32, name="mean_sq", tag="bank")
            for bank, at in ((means[(piece, span)], 0), (mean_sqs[(piece, span)], PIECE)):
                nc.tensor.matmul(
                    bank[:], averaging_matrix[:], part[:, at + lo : at + hi], start=first, stop=last
                )

        def deviation(piece, span):
            width = span[1] - span[0]
            sq_mean = stats.tile([P, width], F32, name="sq_mean")
            nc.scalar.activation(sq_mean[:], means[(piece, span)][:], FUNC.Square)
            var = stats.tile([P, width], F32, name="var")
            nc.vector.tensor_tensor(var[:], mean_sqs[(piece, span)][:], sq_mean[:], SUB)
            rstd = stats.tile([P, width], F32, name="rstd")
            nc.scalar.activation(rstd[:], var[:], FUNC.Abs_reciprocal_sqrt, bias=eps[:])
            rstds[(piece, span)] = rstd

        def normalise(piece, span, blocks):
            lo, hi = span
            centred_tiles = {}
            for b in blocks:
                centred = centred_pool.tile([P, hi - lo], F32, name="centred")
                nc.vector.tensor_tensor(
                    centred[:], pair_tiles[(piece, b)][:, lo:hi], means[(piece, span)][:], SUB
                )
                centred_tiles[b] = centred
            for b in blocks:
                centred = centred_tiles[b]
                nc.vector.tensor_tensor(centred[:], centred[:], rstds[(piece, span)][:], MULT)
                if lo == 0:
                    h_tiles[(piece, b)] = hs_pool.tile([P, PIECE], BF16, name="h")
                nc.scalar.activation(
                    h_tiles[(piece, b)][:, lo:hi], centred[:], FUNC.Identity,
                    bias=shift[:, b : b + 1], scale=gain[:, b : b + 1],
                )

        def accumulate(piece, span, row_blocks, banks, side_by_side):
            lo, hi = span
            if side_by_side:
                order = [(m, b) for b in range(CB) for m in row_blocks]
            else:
                order = [(m, b) for m in row_blocks for b in range(CB)]
            for m, b in order:
                w_tile = weights[m // CB][b // HALF_CB]
                nc.tensor.matmul(
                    banks[m][:, lo:hi], w_tile[:, b % HALF_CB, (m % CB) * P : (m % CB + 1) * P],
                    h_tiles[(piece, b)][:, lo:hi], start=(b == 0), stop=(b == CB - 1),
                )

        def empty(piece, row_blocks, banks):
            for m in row_blocks:
                staged = staging.tile([P, PIECE], F32, name="staged")
                nc.scalar.activation(staged[:], banks[m][:], FUNC.Identity, bias=bias[:, m : m + 1])
                nc.sync.dma_start(out[C + m * P : C + (m + 1) * P, piece_cols(piece)], staged[:])

        def groups_of(piece):
            first = FIRST_GROUP if piece == 0 else GROUP
            return [range(0, first)] + [range(m, m + GROUP) for m in range(first, ROW_BLOCKS, GROUP)]

        def share(step):
            return range(max(step * SHARE, 0), min((step + 1) * SHARE, CB))

        for b in range(CB):
            for span in spans_of(0):
                look_up(0, span, range(b, b + 1))
                average(0, span, averaging, pair_tiles[(0, b)], first=(b == 0), last=(b == CB - 1))
        load_act(1)
        load_weights(wk, "wk_tile")
        load_weights(wv, "wv_tile")
        for span in spans_of(0):
            deviation(0, span)
            for step in range(SHARES):
                normalise(0, span, share(step))

        for piece in range(PIECES):
            following = piece + 1
            groups = groups_of(piece)
            for step, row_blocks in enumerate(groups):
                if following < PIECES and step == NORM_FROM:
                    for i, part in enumerate(split_totals[following]):
                        average(following, WHOLE, averaging_bf, part, first=(i == 0), last=(i == 1))
                    deviation(following, WHOLE)
                if following + 1 < PIECES and step == NORM_FROM:
                    load_act(following + 1)
                banks = {m: psum.tile([P, PIECE], F32, name="bank", tag="bank") for m in row_blocks}
                for span in spans_of(piece) if step == 0 else [WHOLE]:
                    accumulate(piece, span, row_blocks, banks, side_by_side=(step == 0))
                if following < PIECES:
                    look_up(following, WHOLE, share(step))
                    add_up(following, share(step - 1))
                    normalise(following, WHOLE, share(step - NORM_FROM))
                    if step == len(groups) - 1:
                        for late in range(len(groups), NORM_FROM + SHARES):
                            normalise(following, WHOLE, share(late - NORM_FROM))
                empty(piece, row_blocks, banks)
